import numpy as np
import ml_dtypes


def mxq(x, axis, fmt="e4m3"):
    dtype, down = {"e4m3": (ml_dtypes.float8_e4m3fn, 7), "e5m2": (ml_dtypes.float8_e5m2, 14)}[fmt]
    v = np.moveaxis(np.asarray(x, np.float32).astype(ml_dtypes.bfloat16).astype(np.float64), axis, -1)
    blocks = v.reshape(v.shape[:-1] + (-1, 32))
    amax = np.abs(blocks).max(-1, keepdims=True)
    byte = np.maximum(np.where(amax > 0, np.frexp(amax)[1] - 1 + 127, 0) - down, 1)
    scale = np.exp2(byte - 127.0)
    codes = (blocks / scale).astype(np.float32).astype(dtype).astype(np.float64)
    return np.moveaxis((codes * scale).reshape(v.shape), -1, axis)


WIDE = False


def mx_kscale(k):
    if not WIDE:
        return np.ones(k)
    levels = np.array([30, -30])
    if k % 512:
        return np.exp2(np.random.permutation(np.resize(levels, k // 32))).repeat(32)
    a = np.empty((k // 512, 16))
    for p in range(k // 512):
        a[p, :8] = np.random.permutation(np.resize(levels, 8))
        for g in range(8):
            far = levels[np.abs(levels - a[p, g]) >= 10]
            a[p, g + 8] = far[np.random.randint(len(far))]
    return np.exp2(a.ravel()).repeat(32)


BF16 = ml_dtypes.bfloat16


def bf(x):
    return np.asarray(x, np.float32).astype(BF16)


def f64(x):
    return np.asarray(x).astype(np.float64)


B, N, D, F, C, L = 1024, 4096, 1024, 1024, 128, 28
EPS = 1e-12


def l2norm(x):
    n = np.sqrt(np.sum(x * x, axis=1, keepdims=True))
    return x / np.maximum(n, EPS)


def setup_inputs():
    s = mx_kscale(D)
    return {"features": bf(np.random.standard_normal((B, D)) * s),
            "ex_features": bf(np.random.standard_normal((N, D)) * s),
            "g_weight": bf(np.random.standard_normal((F, D)) / np.sqrt(D) / s)}


def reference(features, ex_features, g_weight):
    gq = mxq(f64(g_weight), 1, "e5m2")
    f = mxq(f64(features), 1, "e5m2") @ gq.T
    exf = mxq(f64(ex_features), 1, "e5m2") @ gq.T
    return l2norm(f), l2norm(exf)

@@ -1,0 +1,204 @@
+from contextlib import ExitStack
+
+import concourse.mybir as mybir
+from concourse.masks import make_identity
+
+F32 = mybir.dt.float32
+BF16 = mybir.dt.bfloat16
+U32 = mybir.dt.uint32
+U8 = mybir.dt.uint8
+E5X4 = mybir.dt.float8_e5m2_x4
+ACT = mybir.ActivationFunctionType
+ALU = mybir.AluOpType
+
+P = 128
+K = 1024
+F = 1024
+NH = 512
+ROWS = 5120
+FLOPS = 2 * ROWS * K * F
+EPS2 = 1e-24
+N_PAIRS = ROWS // 256
+PREFETCH = 4
+
+
+def tile_minerva_old_pa_kernel(tc, features, ex_features, g_weight, out_0, out_1):
+    nc = tc.nc
+    with ExitStack() as ctx:
+        const = ctx.enter_context(tc.tile_pool(name="const", bufs=1))
+        wpool = ctx.enter_context(tc.tile_pool(name="wpool", bufs=1))
+        xpool = ctx.enter_context(tc.tile_pool(name="xpool", bufs=1))
+        qpool = ctx.enter_context(tc.tile_pool(name="qpool", bufs=3))
+        small = ctx.enter_context(tc.tile_pool(name="small", bufs=6))
+        junkp = ctx.enter_context(tc.tile_pool(name="junkp", bufs=2))
+        outp = ctx.enter_context(tc.tile_pool(name="outp", bufs=5))
+        tpsum = ctx.enter_context(tc.psum_pool(name="tpsum", bufs=2))
+        mpsum = ctx.enter_context(tc.psum_pool(name="mpsum", bufs=6))
+
+        ident = const.tile([P, P], F32, name="ident")
+        make_identity(nc, ident[:])
+        neg_half = const.tile([P, 1], F32, name="neg_half")
+        nc.gpsimd.memset(neg_half[:], -0.5)
+        warm = const.tile([P, 1], F32, name="warm")
+        nc.scalar.activation(out=warm[:], in_=neg_half[:], func=ACT.Square)
+
+        fv = features.rearrange("(a p j) k -> a p j k", p=P, j=4)
+        ev = ex_features.rearrange("(a p j) k -> a p j k", p=P, j=4)
+        o0 = out_0.rearrange("(a p j) f -> a p j f", p=P, j=4)
+        o1 = out_1.rearrange("(a p j) f -> a p j f", p=P, j=4)
+        n_f = fv.shape[0]
+        n_groups = n_f + ev.shape[0]
+
+        def src_group(a):
+            return fv[a, :, :, :] if a < n_f else ev[a - n_f, :, :, :]
+
+        def dst_group(a):
+            return o0[a, :, :, :] if a < n_f else o1[a - n_f, :, :, :]
+
+        ctx.enter_context(tc.manual_schedule())
+
+        w_raw = []
+        x_raw = {}
+
+        def load_w(f):
+            t = wpool.tile([P, K], BF16, name="w_raw%d" % f)
+            nc.sync.dma_start(out=t[:], in_=g_weight[f * P:(f + 1) * P, :])
+            w_raw.append(t)
+
+        def load_x(a, halves):
+            for h in halves:
+                lo, hi = h
+                t = xpool.tile([P, hi - lo, K], BF16, name="x_raw%d_%d" % (a, lo))
+                nc.sync.dma_start(out=t[:], in_=src_group(a)[:, lo:hi, :])
+                for s in range(lo, hi):
+                    x_raw[(a, s)] = t[:, s - lo, :]
+
+        def transpose_rows(bank, rows):
+            words = rows.bitcast(F32)
+            for g in range(2):
+                for u in range(2):
+                    c = (2 * g + u) * P
+                    nc.tensor.transpose(bank[:, c:c + P], words[:, 256 * g + u:256 * (g + 1):2], ident[:])
+
+        def copy_out(on_scalar, dst, bank):
+            src = bank[:].rearrange("p (g u r) -> p g r u", g=2, u=2)
+            if on_scalar:
+                nc.scalar.copy(out=dst, in_=src)
+            else:
+                nc.vector.tensor_copy(out=dst, in_=src)
+
+        wg = [wpool.tile([P, 2, NH, 4], BF16, name="wg%d" % n, align_bytes=64) for n in range(2)]
+        wc = [wpool.tile([P, 2 * NH], U32, name="wc%d" % n, align_bytes=64) for n in range(2)]
+        ws = [wpool.tile([P, 2 * NH], U8, name="ws%d" % n, align_bytes=64) for n in range(2)]
+
+        def prep_w(n):
+            for q in range(4):
+                f = 4 * n + q
+                bank = mpsum.tile([P, NH], F32, name="mm")
+                transpose_rows(bank, w_raw[f][:])
+                copy_out(q % 2 == 0, wg[n][:, :, q * P:(q + 1) * P, :].bitcast(F32), bank)
+            nc.vector.quantize_mx(
+                out=wc[n][:].bitcast(E5X4),
+                scales=ws[n][:],
+                in_=wg[n][:].rearrange("p g c t -> p (g c t)"),
+            )
+
+        xg = {}
+        xq = {}
+        banks = {}
+        rs = {}
+        ots = {}
+
+        def t_step(j):
+            g_t = qpool.tile([P, 2, 2, P, 4], BF16, name="xg", align_bytes=64)
+            xg[j] = g_t
+            for i in range(2):
+                bank = tpsum.tile([P, NH], F32, name="tb")
+                transpose_rows(bank, x_raw[(j // 2, 2 * (j % 2) + i)])
+                copy_out(i == 0 or j % 2 == 1, g_t[:, i, :, :, :].bitcast(F32), bank)
+
+        def q_step(j):
+            c_t = qpool.tile([P, 4 * P], U32, name="xc", align_bytes=64)
+            s_t = qpool.tile([P, 4 * P], U8, name="xs", align_bytes=64)
+            nc.vector.quantize_mx(
+                out=c_t[:].bitcast(E5X4),
+                scales=s_t[:],
+                in_=xg[j][:].rearrange("p i g r t -> p (i g r t)"),
+            )
+            xq[j] = (c_t, s_t)
+
+        def m_step(j):
+            c_t, s_t = xq[j]
+            for i in range(2):
+                for n in range(2):
+                    bank = mpsum.tile([P, NH], F32, name="mm")
+                    banks[(j, i, n)] = bank
+                    for g in range(2):
+                        cols = slice((2 * i + g) * P, (2 * i + g + 1) * P)
+                        nc.tensor.matmul_mx(
+                            out=bank[:],
+                            lhsT=c_t[:, cols].bitcast(E5X4),
+                            lhsT_scale=s_t[:, cols],
+                            rhs=wc[n][:, g * NH:(g + 1) * NH].bitcast(E5X4),
+                            rhs_scale=ws[n][:, g * NH:(g + 1) * NH],
+                            start=(g == 0),
+                            stop=(g == 1),
+                        )
+
+        def norm_step(j, i):
+            acc = small.tile([P, 2], F32, name="acc")
+            for n in range(2):
+                junk = junkp.tile([P, NH], F32, name="junk")
+                nc.scalar.activation(out=junk[:], in_=banks[(j, i, n)][:], func=ACT.Square, accum_out=acc[:, n:n + 1])
+            n2 = small.tile([P, 1], F32, name="n2")
+            nc.gpsimd.tensor_scalar(out=n2[:], in0=acc[:, 0:1], scalar1=acc[:, 1:2], scalar2=EPS2, op0=ALU.add, op1=ALU.max)
+            r = small.tile([P, 1], F32, name="r")
+            nc.gpsimd.tensor_tensor(out=r[:], in0=n2[:], in1=neg_half[:], op=ALU.pow)
+            rs[(j, i)] = r
+
+        def scale_step(j, i, on_scalar):
+            if i == 0:
+                ots[j] = outp.tile([P, 2, F], F32, name="ot")
+            for n in range(2):
+                dst = ots[j][:, i, n * NH:(n + 1) * NH]
+                if on_scalar[n]:
+                    nc.scalar.activation(out=dst, in_=banks[(j, i, n)][:], func=ACT.Copy, scale=rs[(j, i)][:, 0:1])
+                else:
+                    nc.vector.tensor_scalar(out=dst, in0=banks[(j, i, n)][:], scalar1=rs[(j, i)][:, 0:1], scalar2=None, op0=ALU.mult)
+
+        def store(j, lo, hi):
+            s0 = 2 * (j % 2)
+            nc.sync.dma_start(out=dst_group(j // 2)[:, s0 + lo:s0 + hi, :], in_=ots[j][:, lo:hi, :])
+
+        for f in range(4):
+            load_w(f)
+        load_x(0, [(0, 2)])
+        for f in range(4, 8):
+            load_w(f)
+        load_x(0, [(2, 4)])
+        for a in range(1, PREFETCH):
+            load_x(a, [(0, 4)])
+
+        prep_w(0)
+        t_step(0)
+        q_step(0)
+        prep_w(1)
+
+        for j in range(N_PAIRS):
+            if j + 1 < N_PAIRS:
+                t_step(j + 1)
+            if j >= 1:
+                scale_step(j - 1, 1, (False, False))
+                store(j - 1, 0, 2)
+            if PREFETCH + j < n_groups:
+                load_x(PREFETCH + j, [(0, 4)])
+            if j + 1 < N_PAIRS:
+                q_step(j + 1)
+            m_step(j)
+            norm_step(j, 0)
+            norm_step(j, 1)
+            scale_step(j, 0, (False, False))
+        last = N_PAIRS - 1
+        store(last, 0, 1)
+        scale_step(last, 1, (False, True))
+        store(last, 1, 2)

@@ -20,6 +20,11 @@ FLOPS = 2 * ROWS * K * F
 EPS2 = 1e-24
 N_PAIRS = ROWS // 256
 PREFETCH = 4
+DUM0 = 5
+DUMW = 1
+DUMT = 1
+SHUFFLE_FROM = 99
+AHEAD = 2
 
 
 def tile_minerva_old_pa_kernel(tc, features, ex_features, g_weight, out_0, out_1):
@@ -28,6 +33,7 @@ def tile_minerva_old_pa_kernel(tc, features, ex_features, g_weight, out_0, out_1
         const = ctx.enter_context(tc.tile_pool(name="const", bufs=1))
         wpool = ctx.enter_context(tc.tile_pool(name="wpool", bufs=1))
         xpool = ctx.enter_context(tc.tile_pool(name="xpool", bufs=1))
+        spool = ctx.enter_context(tc.tile_pool(name="spool", bufs=4))
         qpool = ctx.enter_context(tc.tile_pool(name="qpool", bufs=3))
         small = ctx.enter_context(tc.tile_pool(name="small", bufs=6))
         junkp = ctx.enter_context(tc.tile_pool(name="junkp", bufs=2))
@@ -35,6 +41,8 @@ def tile_minerva_old_pa_kernel(tc, features, ex_features, g_weight, out_0, out_1
         tpsum = ctx.enter_context(tc.psum_pool(name="tpsum", bufs=2))
         mpsum = ctx.enter_context(tc.psum_pool(name="mpsum", bufs=6))
 
+        zeros = const.tile([P, NH], BF16, name="zeros")
+        nc.vector.memset(zeros[:], 0.0)
         ident = const.tile([P, P], F32, name="ident")
         make_identity(nc, ident[:])
         neg_half = const.tile([P, 1], F32, name="neg_half")
@@ -59,6 +67,8 @@ def tile_minerva_old_pa_kernel(tc, features, ex_features, g_weight, out_0, out_1
 
         w_raw = []
         x_raw = {}
+        x_pair = {}
+        x_shuf = {}
 
         def load_w(f):
             t = wpool.tile([P, K], BF16, name="w_raw%d" % f)
@@ -72,6 +82,14 @@ def tile_minerva_old_pa_kernel(tc, features, ex_features, g_weight, out_0, out_1
                 nc.sync.dma_start(out=t[:], in_=src_group(a)[:, lo:hi, :])
                 for s in range(lo, hi):
                     x_raw[(a, s)] = t[:, s - lo, :]
+                for s in range(lo, hi, 2):
+                    x_pair[2 * a + s // 2] = t[:, s - lo:s - lo + 2, :]
+
+        dbank = mpsum.tile([P, NH], F32, name="mm")
+
+        def dummies(count):
+            for d in range(count):
+                nc.tensor.matmul(out=dbank[:], lhsT=zeros[:, 0:P], rhs=zeros[:], start=True, stop=True)
 
         def transpose_rows(bank, rows):
             words = rows.bitcast(F32)
@@ -79,6 +97,10 @@ def tile_minerva_old_pa_kernel(tc, features, ex_features, g_weight, out_0, out_1
                 for u in range(2):
                     c = (2 * g + u) * P
                     nc.tensor.transpose(bank[:, c:c + P], words[:, 256 * g + u:256 * (g + 1):2], ident[:])
+
+        def transpose_shuffled(bank, sh, i):
+            for gu in range(4):
+                nc.tensor.transpose(bank[:, gu * P:(gu + 1) * P], sh[:, 4 * i + gu, :], ident[:])
 
         def copy_out(on_scalar, dst, bank):
             src = bank[:].rearrange("p (g u r) -> p g r u", g=2, u=2)
@@ -88,20 +110,28 @@ def tile_minerva_old_pa_kernel(tc, features, ex_features, g_weight, out_0, out_1
                 nc.vector.tensor_copy(out=dst, in_=src)
 
         wg = [wpool.tile([P, 2, NH, 4], BF16, name="wg%d" % n, align_bytes=64) for n in range(2)]
-        wc = [wpool.tile([P, 2 * NH], U32, name="wc%d" % n, align_bytes=64) for n in range(2)]
-        ws = [wpool.tile([P, 2 * NH], U8, name="ws%d" % n, align_bytes=64) for n in range(2)]
+        wc = [wpool.tile([P, 2, NH], U32, name="wc%d" % n, align_bytes=64) for n in range(2)]
+        ws = [wpool.tile([P, 2, NH], U8, name="ws%d" % n, align_bytes=64) for n in range(2)]
+
+        def quant_w(n, q):
+            cols = slice(q * P, (q + 1) * P)
+            for g in range(2):
+                nc.vector.quantize_mx(
+                    out=wc[n][:, g, cols].bitcast(E5X4),
+                    scales=ws[n][:, g, cols],
+                    in_=wg[n][:, g, cols, :].rearrange("p c t -> p (c t)"),
+                )
 
         def prep_w(n):
             for q in range(4):
                 f = 4 * n + q
                 bank = mpsum.tile([P, NH], F32, name="mm")
                 transpose_rows(bank, w_raw[f][:])
+                dummies(DUMW)
                 copy_out(q % 2 == 0, wg[n][:, :, q * P:(q + 1) * P, :].bitcast(F32), bank)
-            nc.vector.quantize_mx(
-                out=wc[n][:].bitcast(E5X4),
-                scales=ws[n][:],
-                in_=wg[n][:].rearrange("p g c t -> p (g c t)"),
-            )
+                if q >= 1:
+                    quant_w(n, q - 1)
+            quant_w(n, 3)
 
         xg = {}
         xq = {}
@@ -109,12 +139,25 @@ def tile_minerva_old_pa_kernel(tc, features, ex_features, g_weight, out_0, out_1
         rs = {}
         ots = {}
 
+        def shuffle_step(j):
+            if j < SHUFFLE_FROM or j >= N_PAIRS:
+                return
+            sh = spool.tile([P, 8, P], F32, name="sh")
+            src = x_pair[j].bitcast(F32).rearrange("p i (g w u) -> p (i g) u w", g=2, u=2)
+            nc.gpsimd.tensor_copy(out=sh[:].rearrange("p (a u) w -> p a u w", u=2), in_=src)
+            x_shuf[j] = sh
+
         def t_step(j):
             g_t = qpool.tile([P, 2, 2, P, 4], BF16, name="xg", align_bytes=64)
             xg[j] = g_t
             for i in range(2):
                 bank = tpsum.tile([P, NH], F32, name="tb")
-                transpose_rows(bank, x_raw[(j // 2, 2 * (j % 2) + i)])
+                if j in x_shuf:
+                    transpose_shuffled(bank, x_shuf[j], i)
+                else:
+                    transpose_rows(bank, x_raw[(j // 2, 2 * (j % 2) + i)])
+                if j < 2:
+                    dummies(DUMT)
                 copy_out(i == 0 or j % 2 == 1, g_t[:, i, :, :, :].bitcast(F32), bank)
 
         def q_step(j):
@@ -139,8 +182,8 @@ def tile_minerva_old_pa_kernel(tc, features, ex_features, g_weight, out_0, out_1
                             out=bank[:],
                             lhsT=c_t[:, cols].bitcast(E5X4),
                             lhsT_scale=s_t[:, cols],
-                            rhs=wc[n][:, g * NH:(g + 1) * NH].bitcast(E5X4),
-                            rhs_scale=ws[n][:, g * NH:(g + 1) * NH],
+                            rhs=wc[n][:, g, :].bitcast(E5X4),
+                            rhs_scale=ws[n][:, g, :],
                             start=(g == 0),
                             stop=(g == 1),
                         )
@@ -179,10 +222,13 @@ def tile_minerva_old_pa_kernel(tc, features, ex_features, g_weight, out_0, out_1
         for a in range(1, PREFETCH):
             load_x(a, [(0, 4)])
 
+        dummies(DUM0)
         prep_w(0)
         t_step(0)
         q_step(0)
         prep_w(1)
+        for j in range(AHEAD + 1):
+            shuffle_step(j)
 
         for j in range(N_PAIRS):
             if j + 1 < N_PAIRS:
@@ -194,6 +240,7 @@ def tile_minerva_old_pa_kernel(tc, features, ex_features, g_weight, out_0, out_1
                 load_x(PREFETCH + j, [(0, 4)])
             if j + 1 < N_PAIRS:
                 q_step(j + 1)
+            shuffle_step(j + 1 + AHEAD)
             m_step(j)
             norm_step(j, 0)
             norm_step(j, 1)

@@ -19,12 +19,16 @@ ROWS = 5120
 FLOPS = 2 * ROWS * K * F
 EPS2 = 1e-24
 N_PAIRS = ROWS // 256
-PREFETCH = 4
-DUM0 = 5
-DUMW = 1
-DUMT = 1
-SHUFFLE_FROM = 99
+PREFETCH = 6
 AHEAD = 2
+
+
+def copy_on_scalar(j, i):
+    return not (i == 0 and j % 2 == 0)
+
+
+def shuffled(j, i):
+    return False
 
 
 def tile_minerva_old_pa_kernel(tc, features, ex_features, g_weight, out_0, out_1):
@@ -37,12 +41,10 @@ def tile_minerva_old_pa_kernel(tc, features, ex_features, g_weight, out_0, out_1
         qpool = ctx.enter_context(tc.tile_pool(name="qpool", bufs=3))
         small = ctx.enter_context(tc.tile_pool(name="small", bufs=6))
         junkp = ctx.enter_context(tc.tile_pool(name="junkp", bufs=2))
-        outp = ctx.enter_context(tc.tile_pool(name="outp", bufs=5))
+        outp = ctx.enter_context(tc.tile_pool(name="outp", bufs=6))
         tpsum = ctx.enter_context(tc.psum_pool(name="tpsum", bufs=2))
         mpsum = ctx.enter_context(tc.psum_pool(name="mpsum", bufs=6))
 
-        zeros = const.tile([P, NH], BF16, name="zeros")
-        nc.vector.memset(zeros[:], 0.0)
         ident = const.tile([P, P], F32, name="ident")
         make_identity(nc, ident[:])
         neg_half = const.tile([P, 1], F32, name="neg_half")
@@ -67,7 +69,6 @@ def tile_minerva_old_pa_kernel(tc, features, ex_features, g_weight, out_0, out_1
 
         w_raw = []
         x_raw = {}
-        x_pair = {}
         x_shuf = {}
 
         def load_w(f):
@@ -82,14 +83,6 @@ def tile_minerva_old_pa_kernel(tc, features, ex_features, g_weight, out_0, out_1
                 nc.sync.dma_start(out=t[:], in_=src_group(a)[:, lo:hi, :])
                 for s in range(lo, hi):
                     x_raw[(a, s)] = t[:, s - lo, :]
-                for s in range(lo, hi, 2):
-                    x_pair[2 * a + s // 2] = t[:, s - lo:s - lo + 2, :]
-
-        dbank = mpsum.tile([P, NH], F32, name="mm")
-
-        def dummies(count):
-            for d in range(count):
-                nc.tensor.matmul(out=dbank[:], lhsT=zeros[:, 0:P], rhs=zeros[:], start=True, stop=True)
 
         def transpose_rows(bank, rows):
             words = rows.bitcast(F32)
@@ -98,9 +91,9 @@ def tile_minerva_old_pa_kernel(tc, features, ex_features, g_weight, out_0, out_1
                     c = (2 * g + u) * P
                     nc.tensor.transpose(bank[:, c:c + P], words[:, 256 * g + u:256 * (g + 1):2], ident[:])
 
-        def transpose_shuffled(bank, sh, i):
+        def transpose_shuffled(bank, sh):
             for gu in range(4):
-                nc.tensor.transpose(bank[:, gu * P:(gu + 1) * P], sh[:, 4 * i + gu, :], ident[:])
+                nc.tensor.transpose(bank[:, gu * P:(gu + 1) * P], sh[:, gu, :], ident[:])
 
         def copy_out(on_scalar, dst, bank):
             src = bank[:].rearrange("p (g u r) -> p g r u", g=2, u=2)
@@ -127,7 +120,6 @@ def tile_minerva_old_pa_kernel(tc, features, ex_features, g_weight, out_0, out_1
                 f = 4 * n + q
                 bank = mpsum.tile([P, NH], F32, name="mm")
                 transpose_rows(bank, w_raw[f][:])
-                dummies(DUMW)
                 copy_out(q % 2 == 0, wg[n][:, :, q * P:(q + 1) * P, :].bitcast(F32), bank)
                 if q >= 1:
                     quant_w(n, q - 1)
@@ -140,25 +132,28 @@ def tile_minerva_old_pa_kernel(tc, features, ex_features, g_weight, out_0, out_1
         ots = {}
 
         def shuffle_step(j):
-            if j < SHUFFLE_FROM or j >= N_PAIRS:
+            if j >= N_PAIRS:
                 return
-            sh = spool.tile([P, 8, P], F32, name="sh")
-            src = x_pair[j].bitcast(F32).rearrange("p i (g w u) -> p (i g) u w", g=2, u=2)
-            nc.gpsimd.tensor_copy(out=sh[:].rearrange("p (a u) w -> p a u w", u=2), in_=src)
-            x_shuf[j] = sh
+            for i in range(2):
+                if shuffled(j, i):
+                    sh = spool.tile([P, 4, P], F32, name="sh")
+                    src = x_raw[(j // 2, 2 * (j % 2) + i)].bitcast(F32).rearrange("p (g w u) -> p g u w", g=2, u=2)
+                    nc.vector.tensor_copy(out=sh[:].rearrange("p (g u) w -> p g u w", u=2), in_=src)
+                    x_shuf[(j, i)] = sh
 
         def t_step(j):
             g_t = qpool.tile([P, 2, 2, P, 4], BF16, name="xg", align_bytes=64)
             xg[j] = g_t
+            tbs = []
             for i in range(2):
                 bank = tpsum.tile([P, NH], F32, name="tb")
-                if j in x_shuf:
-                    transpose_shuffled(bank, x_shuf[j], i)
+                if (j, i) in x_shuf:
+                    transpose_shuffled(bank, x_shuf[(j, i)])
                 else:
                     transpose_rows(bank, x_raw[(j // 2, 2 * (j % 2) + i)])
-                if j < 2:
-                    dummies(DUMT)
-                copy_out(i == 0 or j % 2 == 1, g_t[:, i, :, :, :].bitcast(F32), bank)
+                tbs.append(bank)
+            for i in range(2):
+                copy_out(copy_on_scalar(j, i), g_t[:, i, :, :, :].bitcast(F32), tbs[i])
 
         def q_step(j):
             c_t = qpool.tile([P, 4 * P], U32, name="xc", align_bytes=64)
@@ -222,24 +217,22 @@ def tile_minerva_old_pa_kernel(tc, features, ex_features, g_weight, out_0, out_1
         for a in range(1, PREFETCH):
             load_x(a, [(0, 4)])
 
-        dummies(DUM0)
         prep_w(0)
         t_step(0)
         q_step(0)
         prep_w(1)
-        for j in range(AHEAD + 1):
+        for j in range(1, AHEAD + 1):
             shuffle_step(j)
 
         for j in range(N_PAIRS):
             if j + 1 < N_PAIRS:
                 t_step(j + 1)
+                q_step(j + 1)
             if j >= 1:
                 scale_step(j - 1, 1, (False, False))
                 store(j - 1, 0, 2)
             if PREFETCH + j < n_groups:
                 load_x(PREFETCH + j, [(0, 4)])
-            if j + 1 < N_PAIRS:
-                q_step(j + 1)
             shuffle_step(j + 1 + AHEAD)
             m_step(j)
             norm_step(j, 0)

@@ -24,11 +24,11 @@ AHEAD = 2
 
 
 def copy_on_scalar(j, i):
-    return not (i == 0 and j % 2 == 0)
+    return True
 
 
 def shuffled(j, i):
-    return False
+    return j >= 3 and i == 1
 
 
 def tile_minerva_old_pa_kernel(tc, features, ex_features, g_weight, out_0, out_1):

@@ -21,6 +21,7 @@ EPS2 = 1e-24
 N_PAIRS = ROWS // 256
 PREFETCH = 6
 AHEAD = 2
+W_PAIRS = (0, 1, 2, 1)
 
 
 def copy_on_scalar(j, i):
@@ -42,8 +43,7 @@ def tile_minerva_old_pa_kernel(tc, features, ex_features, g_weight, out_0, out_1
         small = ctx.enter_context(tc.tile_pool(name="small", bufs=6))
         junkp = ctx.enter_context(tc.tile_pool(name="junkp", bufs=2))
         outp = ctx.enter_context(tc.tile_pool(name="outp", bufs=6))
-        tpsum = ctx.enter_context(tc.psum_pool(name="tpsum", bufs=2))
-        mpsum = ctx.enter_context(tc.psum_pool(name="mpsum", bufs=6))
+        psum = ctx.enter_context(tc.psum_pool(name="psum", bufs=1))
 
         ident = const.tile([P, P], F32, name="ident")
         make_identity(nc, ident[:])
@@ -70,6 +70,9 @@ def tile_minerva_old_pa_kernel(tc, features, ex_features, g_weight, out_0, out_1
         w_raw = []
         x_raw = {}
         x_shuf = {}
+
+        def bank_tile(pair, half):
+            return psum.tile([P, NH], F32, name="bank%d" % (2 * (pair % 4) + half))
 
         def load_w(f):
             t = wpool.tile([P, K], BF16, name="w_raw%d" % f)
@@ -118,7 +121,7 @@ def tile_minerva_old_pa_kernel(tc, features, ex_features, g_weight, out_0, out_1
         def prep_w(n):
             for q in range(4):
                 f = 4 * n + q
-                bank = mpsum.tile([P, NH], F32, name="mm")
+                bank = bank_tile(W_PAIRS[f // 2], f % 2)
                 transpose_rows(bank, w_raw[f][:])
                 copy_out(q % 2 == 0, wg[n][:, :, q * P:(q + 1) * P, :].bitcast(F32), bank)
                 if q >= 1:
@@ -146,7 +149,7 @@ def tile_minerva_old_pa_kernel(tc, features, ex_features, g_weight, out_0, out_1
             xg[j] = g_t
             tbs = []
             for i in range(2):
-                bank = tpsum.tile([P, NH], F32, name="tb")
+                bank = bank_tile(j - 1, i)
                 if (j, i) in x_shuf:
                     transpose_shuffled(bank, x_shuf[(j, i)])
                 else:
@@ -169,7 +172,7 @@ def tile_minerva_old_pa_kernel(tc, features, ex_features, g_weight, out_0, out_1
             c_t, s_t = xq[j]
             for i in range(2):
                 for n in range(2):
-                    bank = mpsum.tile([P, NH], F32, name="mm")
+                    bank = bank_tile(j + 2 if i == 0 else j, n)
                     banks[(j, i, n)] = bank
                     for g in range(2):
                         cols = slice((2 * i + g) * P, (2 * i + g + 1) * P)

@@ -25,7 +25,7 @@ W_PAIRS = (0, 1, 2, 1)
 
 
 def copy_on_scalar(j, i):
-    return True
+    return not (i == 1 and j % 2 == 1)
 
 
 def shuffled(j, i):
@@ -230,6 +230,9 @@ def tile_minerva_old_pa_kernel(tc, features, ex_features, g_weight, out_0, out_1
         for j in range(N_PAIRS):
             if j + 1 < N_PAIRS:
                 t_step(j + 1)
+            if j >= 1:
+                scale_step(j - 1, 0, (False, False))
+            if j + 1 < N_PAIRS:
                 q_step(j + 1)
             if j >= 1:
                 scale_step(j - 1, 1, (False, False))
@@ -240,8 +243,8 @@ def tile_minerva_old_pa_kernel(tc, features, ex_features, g_weight, out_0, out_1
             m_step(j)
             norm_step(j, 0)
             norm_step(j, 1)
-            scale_step(j, 0, (False, False))
         last = N_PAIRS - 1
+        scale_step(last, 0, (False, False))
         store(last, 0, 1)
         scale_step(last, 1, (False, True))
         store(last, 1, 2)

@@ -17,7 +17,7 @@ F = 1024
 NH = 512
 ROWS = 5120
 FLOPS = 2 * ROWS * K * F
-EPS2 = 1e-24
+R_MAX = 1e12
 N_PAIRS = ROWS // 256
 PREFETCH = 6
 AHEAD = 2
@@ -47,10 +47,10 @@ def tile_minerva_old_pa_kernel(tc, features, ex_features, g_weight, out_0, out_1
 
         ident = const.tile([P, P], F32, name="ident")
         make_identity(nc, ident[:])
-        neg_half = const.tile([P, 1], F32, name="neg_half")
-        nc.gpsimd.memset(neg_half[:], -0.5)
+        one = const.tile([P, 1], F32, name="one")
+        nc.gpsimd.memset(one[:], 1.0)
         warm = const.tile([P, 1], F32, name="warm")
-        nc.scalar.activation(out=warm[:], in_=neg_half[:], func=ACT.Square)
+        nc.scalar.activation(out=warm[:], in_=one[:], func=ACT.Abs_reciprocal_sqrt)
 
         fv = features.rearrange("(a p j) k -> a p j k", p=P, j=4)
         ev = ex_features.rearrange("(a p j) k -> a p j k", p=P, j=4)
@@ -128,6 +128,15 @@ def tile_minerva_old_pa_kernel(tc, features, ex_features, g_weight, out_0, out_1
                     quant_w(n, q - 1)
             quant_w(n, 3)
 
+        pending = []
+
+        def rsqrt_pending():
+            for (j, i, acc) in pending:
+                r = small.tile([P, 1], F32, name="r")
+                nc.scalar.activation(out=r[:], in_=acc[:, 0:1], func=ACT.Abs_reciprocal_sqrt, bias=acc[:, 1:2])
+                rs[(j, i)] = r
+            pending.clear()
+
         xg = {}
         xq = {}
         banks = {}
@@ -157,6 +166,8 @@ def tile_minerva_old_pa_kernel(tc, features, ex_features, g_weight, out_0, out_1
                 tbs.append(bank)
             for i in range(2):
                 copy_out(copy_on_scalar(j, i), g_t[:, i, :, :, :].bitcast(F32), tbs[i])
+                if i == 0:
+                    rsqrt_pending()
 
         def q_step(j):
             c_t = qpool.tile([P, 4 * P], U32, name="xc", align_bytes=64)
@@ -191,21 +202,22 @@ def tile_minerva_old_pa_kernel(tc, features, ex_features, g_weight, out_0, out_1
             for n in range(2):
                 junk = junkp.tile([P, NH], F32, name="junk")
                 nc.scalar.activation(out=junk[:], in_=banks[(j, i, n)][:], func=ACT.Square, accum_out=acc[:, n:n + 1])
-            n2 = small.tile([P, 1], F32, name="n2")
-            nc.gpsimd.tensor_scalar(out=n2[:], in0=acc[:, 0:1], scalar1=acc[:, 1:2], scalar2=EPS2, op0=ALU.add, op1=ALU.max)
-            r = small.tile([P, 1], F32, name="r")
-            nc.gpsimd.tensor_tensor(out=r[:], in0=n2[:], in1=neg_half[:], op=ALU.pow)
-            rs[(j, i)] = r
+                if n == 0:
+                    rsqrt_pending()
+            pending.append((j, i, acc))
 
-        def scale_step(j, i, on_scalar):
+        def scale_step(j, i):
             if i == 0:
                 ots[j] = outp.tile([P, 2, F], F32, name="ot")
             for n in range(2):
-                dst = ots[j][:, i, n * NH:(n + 1) * NH]
-                if on_scalar[n]:
-                    nc.scalar.activation(out=dst, in_=banks[(j, i, n)][:], func=ACT.Copy, scale=rs[(j, i)][:, 0:1])
-                else:
-                    nc.vector.tensor_scalar(out=dst, in0=banks[(j, i, n)][:], scalar1=rs[(j, i)][:, 0:1], scalar2=None, op0=ALU.mult)
+                nc.vector.scalar_tensor_tensor(
+                    out=ots[j][:, i, n * NH:(n + 1) * NH],
+                    in0=rs[(j, i)][:, 0:1].to_broadcast([P, NH]),
+                    scalar=R_MAX,
+                    in1=banks[(j, i, n)][:],
+                    op0=ALU.min,
+                    op1=ALU.mult,
+                )
 
         def store(j, lo, hi):
             s0 = 2 * (j % 2)
@@ -230,12 +242,14 @@ def tile_minerva_old_pa_kernel(tc, features, ex_features, g_weight, out_0, out_1
         for j in range(N_PAIRS):
             if j + 1 < N_PAIRS:
                 t_step(j + 1)
+            else:
+                rsqrt_pending()
             if j >= 1:
-                scale_step(j - 1, 0, (False, False))
+                scale_step(j - 1, 0)
             if j + 1 < N_PAIRS:
                 q_step(j + 1)
             if j >= 1:
-                scale_step(j - 1, 1, (False, False))
+                scale_step(j - 1, 1)
                 store(j - 1, 0, 2)
             if PREFETCH + j < n_groups:
                 load_x(PREFETCH + j, [(0, 4)])
@@ -244,7 +258,8 @@ def tile_minerva_old_pa_kernel(tc, features, ex_features, g_weight, out_0, out_1
             norm_step(j, 0)
             norm_step(j, 1)
         last = N_PAIRS - 1
-        scale_step(last, 0, (False, False))
+        rsqrt_pending()
+        scale_step(last, 0)
         store(last, 0, 1)
-        scale_step(last, 1, (False, True))
+        scale_step(last, 1)
         store(last, 1, 2)

@@ -38,7 +38,7 @@ def tile_minerva_old_pa_kernel(tc, features, ex_features, g_weight, out_0, out_1
         const = ctx.enter_context(tc.tile_pool(name="const", bufs=1))
         wpool = ctx.enter_context(tc.tile_pool(name="wpool", bufs=1))
         xpool = ctx.enter_context(tc.tile_pool(name="xpool", bufs=1))
-        spool = ctx.enter_context(tc.tile_pool(name="spool", bufs=4))
+        slots = ctx.enter_context(tc.tile_pool(name="slots", bufs=1))
         qpool = ctx.enter_context(tc.tile_pool(name="qpool", bufs=3))
         small = ctx.enter_context(tc.tile_pool(name="small", bufs=6))
         junkp = ctx.enter_context(tc.tile_pool(name="junkp", bufs=2))
@@ -148,13 +148,15 @@ def tile_minerva_old_pa_kernel(tc, features, ex_features, g_weight, out_0, out_1
                 return
             for i in range(2):
                 if shuffled(j, i):
-                    sh = spool.tile([P, 4, P], F32, name="sh")
-                    src = x_raw[(j // 2, 2 * (j % 2) + i)].bitcast(F32).rearrange("p (g w u) -> p g u w", g=2, u=2)
-                    nc.vector.tensor_copy(out=sh[:].rearrange("p (g u) w -> p g u w", u=2), in_=src)
+                    sh = slots.tile([P, 4, P], F32, name="slot%d" % ((j - 2) % 3), align_bytes=64)
+                    src = x_raw[(j // 2, 2 * (j % 2) + i)].rearrange("p (g w u e) -> p g u w e", g=2, u=2, e=2)
+                    dst = sh[:].rearrange("p s w -> p (s w)").bitcast(BF16).rearrange("p (g u w e) -> p g u w e", g=2, u=2, e=2)
+                    for g in range(2):
+                        nc.gpsimd.tensor_scalar(out=dst[:, g, :, :, :], in0=src[:, g, :, :, :], scalar1=1.0, scalar2=0.0, op0=ALU.mult, op1=ALU.add)
                     x_shuf[(j, i)] = sh
 
         def t_step(j):
-            g_t = qpool.tile([P, 2, 2, P, 4], BF16, name="xg", align_bytes=64)
+            g_t = slots.tile([P, 2, 2, P, 4], BF16, name="slot%d" % (j % 3), align_bytes=64)
             xg[j] = g_t
             tbs = []
             for i in range(2):

@@ -28,8 +28,8 @@ def copy_on_scalar(j, i):
     return not (i == 1 and j % 2 == 1)
 
 
-def shuffled(j, i):
-    return j >= 3 and i == 1
+def laid_out(j, i, g):
+    return j >= 3 and (i == 1 or g == 0)
 
 
 def tile_minerva_old_pa_kernel(tc, features, ex_features, g_weight, out_0, out_1):
@@ -94,9 +94,15 @@ def tile_minerva_old_pa_kernel(tc, features, ex_features, g_weight, out_0, out_1
                     c = (2 * g + u) * P
                     nc.tensor.transpose(bank[:, c:c + P], words[:, 256 * g + u:256 * (g + 1):2], ident[:])
 
-        def transpose_shuffled(bank, sh):
-            for gu in range(4):
-                nc.tensor.transpose(bank[:, gu * P:(gu + 1) * P], sh[:, gu, :], ident[:])
+        def transpose_tile(bank, j, i):
+            words = x_raw[(j // 2, 2 * (j % 2) + i)].bitcast(F32)
+            for g in range(2):
+                for u in range(2):
+                    c = (2 * g + u) * P
+                    if laid_out(j, i, g):
+                        nc.tensor.transpose(bank[:, c:c + P], x_shuf[j][:, 4 * i + 2 * g + u, :], ident[:])
+                    else:
+                        nc.tensor.transpose(bank[:, c:c + P], words[:, 256 * g + u:256 * (g + 1):2], ident[:])
 
         def copy_out(on_scalar, dst, bank):
             src = bank[:].rearrange("p (g u r) -> p g r u", g=2, u=2)
@@ -146,14 +152,16 @@ def tile_minerva_old_pa_kernel(tc, features, ex_features, g_weight, out_0, out_1
         def shuffle_step(j):
             if j >= N_PAIRS:
                 return
-            for i in range(2):
-                if shuffled(j, i):
-                    sh = slots.tile([P, 4, P], F32, name="slot%d" % ((j - 2) % 3), align_bytes=64)
-                    src = x_raw[(j // 2, 2 * (j % 2) + i)].rearrange("p (g w u e) -> p g u w e", g=2, u=2, e=2)
-                    dst = sh[:].rearrange("p s w -> p (s w)").bitcast(BF16).rearrange("p (g u w e) -> p g u w e", g=2, u=2, e=2)
-                    for g in range(2):
-                        nc.gpsimd.tensor_scalar(out=dst[:, g, :, :, :], in0=src[:, g, :, :, :], scalar1=1.0, scalar2=0.0, op0=ALU.mult, op1=ALU.add)
-                    x_shuf[(j, i)] = sh
+            if not laid_out(j, 1, 0):
+                return
+            sh = slots.tile([P, 8, P], F32, name="slot%d" % ((j - 2) % 3), align_bytes=64)
+            dst = sh[:].rearrange("p s w -> p (s w)").bitcast(BF16).rearrange("p (i g u w e) -> p i g u w e", i=2, g=2, u=2, e=2)
+            for i in (1, 0):
+                src = x_raw[(j // 2, 2 * (j % 2) + i)].rearrange("p (g w u e) -> p g u w e", g=2, u=2, e=2)
+                for g in range(2):
+                    if laid_out(j, i, g):
+                        nc.gpsimd.tensor_scalar(out=dst[:, i, g, :, :, :], in0=src[:, g, :, :, :], scalar1=1.0, scalar2=0.0, op0=ALU.mult, op1=ALU.add)
+            x_shuf[j] = sh
 
         def t_step(j):
             g_t = slots.tile([P, 2, 2, P, 4], BF16, name="slot%d" % (j % 3), align_bytes=64)
@@ -161,10 +169,7 @@ def tile_minerva_old_pa_kernel(tc, features, ex_features, g_weight, out_0, out_1
             tbs = []
             for i in range(2):
                 bank = bank_tile(j - 1, i)
-                if (j, i) in x_shuf:
-                    transpose_shuffled(bank, x_shuf[(j, i)])
-                else:
-                    transpose_rows(bank, x_raw[(j // 2, 2 * (j % 2) + i)])
+                transpose_tile(bank, j, i)
                 tbs.append(bank)
             for i in range(2):
                 copy_out(copy_on_scalar(j, i), g_t[:, i, :, :, :].bitcast(F32), tbs[i])

@@ -29,7 +29,7 @@ def copy_on_scalar(j, i):
 
 
 def laid_out(j, i, g):
-    return j >= 3 and (i == 1 or g == 0)
+    return j >= 3 and (i == 1 or g == 1)
 
 
 def tile_minerva_old_pa_kernel(tc, features, ex_features, g_weight, out_0, out_1):
@@ -188,21 +188,23 @@ def tile_minerva_old_pa_kernel(tc, features, ex_features, g_weight, out_0, out_1
 
         def m_step(j):
             c_t, s_t = xq[j]
-            for i in range(2):
-                for n in range(2):
-                    bank = bank_tile(j + 2 if i == 0 else j, n)
-                    banks[(j, i, n)] = bank
-                    for g in range(2):
-                        cols = slice((2 * i + g) * P, (2 * i + g + 1) * P)
-                        nc.tensor.matmul_mx(
-                            out=bank[:],
-                            lhsT=c_t[:, cols].bitcast(E5X4),
-                            lhsT_scale=s_t[:, cols],
-                            rhs=wc[n][:, g, :].bitcast(E5X4),
-                            rhs_scale=ws[n][:, g, :],
-                            start=(g == 0),
-                            stop=(g == 1),
-                        )
+            groups = [(i, n) for i in range(2) for n in range(2)]
+            if j == 0:
+                groups = [(i, n) for n in range(2) for i in range(2)]
+            for (i, n) in groups:
+                bank = bank_tile(j + 2 if i == 0 else j, n)
+                banks[(j, i, n)] = bank
+                for g in range(2):
+                    cols = slice((2 * i + g) * P, (2 * i + g + 1) * P)
+                    nc.tensor.matmul_mx(
+                        out=bank[:],
+                        lhsT=c_t[:, cols].bitcast(E5X4),
+                        lhsT_scale=s_t[:, cols],
+                        rhs=wc[n][:, g, :].bitcast(E5X4),
+                        rhs_scale=ws[n][:, g, :],
+                        start=(g == 0),
+                        stop=(g == 1),
+                    )
 
         def norm_step(j, i):
             acc = small.tile([P, 2], F32, name="acc")

@@ -22,6 +22,8 @@ N_PAIRS = ROWS // 256
 PREFETCH = 6
 AHEAD = 2
 W_PAIRS = (0, 1, 2, 1)
+FINE = 16
+ON_SCALAR = ((19, 0, 1), (19, 1, 1))
 
 
 def copy_on_scalar(j, i):
@@ -192,7 +194,7 @@ def tile_minerva_old_pa_kernel(tc, features, ex_features, g_weight, out_0, out_1
             if j == 0:
                 groups = [(i, n) for n in range(2) for i in range(2)]
             for (i, n) in groups:
-                bank = bank_tile(j + 2 if i == 0 else j, n)
+                bank = bank_tile(j + 2 if (i == 0) != (j == N_PAIRS - 1) else j, n)
                 banks[(j, i, n)] = bank
                 for g in range(2):
                     cols = slice((2 * i + g) * P, (2 * i + g + 1) * P)
@@ -218,7 +220,13 @@ def tile_minerva_old_pa_kernel(tc, features, ex_features, g_weight, out_0, out_1
         def scale_step(j, i):
             if i == 0:
                 ots[j] = outp.tile([P, 2, F], F32, name="ot")
+            if any((j, i, n) in ON_SCALAR for n in range(2)):
+                rc = small.tile([P, 1], F32, name="rc")
+                nc.vector.tensor_scalar(out=rc[:], in0=rs[(j, i)][:, 0:1], scalar1=R_MAX, scalar2=None, op0=ALU.min)
             for n in range(2):
+                if (j, i, n) in ON_SCALAR:
+                    nc.scalar.activation(out=ots[j][:, i, n * NH:(n + 1) * NH], in_=banks[(j, i, n)][:], func=ACT.Copy, scale=rc[:, 0:1])
+                    continue
                 nc.vector.scalar_tensor_tensor(
                     out=ots[j][:, i, n * NH:(n + 1) * NH],
                     in0=rs[(j, i)][:, 0:1].to_broadcast([P, NH]),
@@ -255,11 +263,16 @@ def tile_minerva_old_pa_kernel(tc, features, ex_features, g_weight, out_0, out_1
                 rsqrt_pending()
             if j >= 1:
                 scale_step(j - 1, 0)
+                if j >= FINE:
+                    store(j - 1, 0, 1)
             if j + 1 < N_PAIRS:
                 q_step(j + 1)
             if j >= 1:
                 scale_step(j - 1, 1)
-                store(j - 1, 0, 2)
+                if j >= FINE:
+                    store(j - 1, 1, 2)
+                else:
+                    store(j - 1, 0, 2)
             if PREFETCH + j < n_groups:
                 load_x(PREFETCH + j, [(0, 4)])
             shuffle_step(j + 1 + AHEAD)

@@ -77,9 +77,12 @@ def tile_minerva_old_pa_kernel(tc, features, ex_features, g_weight, out_0, out_1
             return psum.tile([P, NH], F32, name="bank%d" % (2 * (pair % 4) + half))
 
         def load_w(f):
-            t = wpool.tile([P, K], BF16, name="w_raw%d" % f)
-            nc.sync.dma_start(out=t[:], in_=g_weight[f * P:(f + 1) * P, :])
-            w_raw.append(t)
+            if f % 2 == 1:
+                return
+            t = wpool.tile([P, 2, K], BF16, name="w_raw%d" % f)
+            nc.sync.dma_start(out=t[:], in_=g_weight[f * P:(f + 2) * P, :].rearrange("(t p) k -> p t k", p=P))
+            w_raw.append(t[:, 0, :])
+            w_raw.append(t[:, 1, :])
 
         def load_x(a, halves):
             for h in halves:
@@ -130,7 +133,7 @@ def tile_minerva_old_pa_kernel(tc, features, ex_features, g_weight, out_0, out_1
             for q in range(4):
                 f = 4 * n + q
                 bank = bank_tile(W_PAIRS[f // 2], f % 2)
-                transpose_rows(bank, w_raw[f][:])
+                transpose_rows(bank, w_raw[f])
                 copy_out(q % 2 == 0, wg[n][:, :, q * P:(q + 1) * P, :].bitcast(F32), bank)
                 if q >= 1:
                     quant_w(n, q - 1)

@@ -72,6 +72,7 @@ def tile_minerva_old_pa_kernel(tc, features, ex_features, g_weight, out_0, out_1
         w_raw = []
         x_raw = {}
         x_shuf = {}
+        x_pair = {}
 
         def bank_tile(pair, half):
             return psum.tile([P, NH], F32, name="bank%d" % (2 * (pair % 4) + half))
@@ -91,6 +92,8 @@ def tile_minerva_old_pa_kernel(tc, features, ex_features, g_weight, out_0, out_1
                 nc.sync.dma_start(out=t[:], in_=src_group(a)[:, lo:hi, :])
                 for s in range(lo, hi):
                     x_raw[(a, s)] = t[:, s - lo, :]
+                    if s % 2 == 0:
+                        x_pair[2 * a + s // 2] = t[:, s - lo:s - lo + 2, :]
 
         def transpose_rows(bank, rows):
             words = rows.bitcast(F32)
@@ -105,7 +108,8 @@ def tile_minerva_old_pa_kernel(tc, features, ex_features, g_weight, out_0, out_1
                 for u in range(2):
                     c = (2 * g + u) * P
                     if laid_out(j, i, g):
-                        nc.tensor.transpose(bank[:, c:c + P], x_shuf[j][:, 4 * i + 2 * g + u, :], ident[:])
+                        w0 = 384 * u + 256 * i + 128 * g - 128
+                        nc.tensor.transpose(bank[:, c:c + P], x_shuf[j][:, w0:w0 + P], ident[:])
                     else:
                         nc.tensor.transpose(bank[:, c:c + P], words[:, 256 * g + u:256 * (g + 1):2], ident[:])
 
@@ -160,13 +164,11 @@ def tile_minerva_old_pa_kernel(tc, features, ex_features, g_weight, out_0, out_1
             if not laid_out(j, 1, 0):
                 return
             sh = slots.tile([P, 8, P], F32, name="slot%d" % ((j - 2) % 3), align_bytes=64)
-            dst = sh[:].rearrange("p s w -> p (s w)").bitcast(BF16).rearrange("p (i g u w e) -> p i g u w e", i=2, g=2, u=2, e=2)
-            for i in (1, 0):
-                src = x_raw[(j // 2, 2 * (j % 2) + i)].rearrange("p (g w u e) -> p g u w e", g=2, u=2, e=2)
-                for g in range(2):
-                    if laid_out(j, i, g):
-                        nc.gpsimd.tensor_scalar(out=dst[:, i, g, :, :, :], in0=src[:, g, :, :, :], scalar1=1.0, scalar2=0.0, op0=ALU.mult, op1=ALU.add)
-            x_shuf[j] = sh
+            words = sh[:].rearrange("p s w -> p (s w)")
+            dst = words[:, 0:768].bitcast(BF16).rearrange("p (u v e) -> p u v e", u=2, e=2)
+            src = x_pair[j].rearrange("p i k -> p (i k)").rearrange("p (v u e) -> p u v e", u=2, e=2)
+            nc.gpsimd.tensor_scalar(out=dst, in0=src[:, :, 128:512, :], scalar1=1.0, scalar2=0.0, op0=ALU.mult, op1=ALU.add)
+            x_shuf[j] = words
 
         def t_step(j):
             g_t = slots.tile([P, 2, 2, P, 4], BF16, name="slot%d" % (j % 3), align_bytes=64)

@@ -75,7 +75,8 @@ def tile_minerva_old_pa_kernel(tc, features, ex_features, g_weight, out_0, out_1
         x_pair = {}
 
         def bank_tile(pair, half):
-            return psum.tile([P, NH], F32, name="bank%d" % (2 * (pair % 4) + half))
+            b = pair % 4 + 4 * half
+            return psum.tile([P, NH], F32, name="bank%d" % b, offset=2048 * b)
 
         def load_w(f):
             if f % 2 == 1:

from contextlib import ExitStack

import concourse.mybir as mybir
from concourse.masks import make_identity

F32 = mybir.dt.float32
BF16 = mybir.dt.bfloat16
U32 = mybir.dt.uint32
U8 = mybir.dt.uint8
E5X4 = mybir.dt.float8_e5m2_x4
ACT = mybir.ActivationFunctionType
ALU = mybir.AluOpType

P = 128
K = 1024
F = 1024
NH = 512
ROWS = 5120
FLOPS = 2 * ROWS * K * F
R_MAX = 1e12
N_PAIRS = ROWS // 256
PREFETCH = 6
AHEAD = 2
W_PAIRS = (0, 1, 2, 1)
FINE = 16
ON_SCALAR = ((19, 0, 1), (19, 1, 1))


def copy_on_scalar(j, i):
    return not (i == 1 and j % 2 == 1)


def laid_out(j, i, g):
    return j >= 3 and (i == 1 or g == 1)


def tile_minerva_old_pa_kernel(tc, features, ex_features, g_weight, out_0, out_1):
    nc = tc.nc
    with ExitStack() as ctx:
        const = ctx.enter_context(tc.tile_pool(name="const", bufs=1))
        wpool = ctx.enter_context(tc.tile_pool(name="wpool", bufs=1))
        xpool = ctx.enter_context(tc.tile_pool(name="xpool", bufs=1))
        slots = ctx.enter_context(tc.tile_pool(name="slots", bufs=1))
        qpool = ctx.enter_context(tc.tile_pool(name="qpool", bufs=3))
        small = ctx.enter_context(tc.tile_pool(name="small", bufs=6))
        junkp = ctx.enter_context(tc.tile_pool(name="junkp", bufs=2))
        outp = ctx.enter_context(tc.tile_pool(name="outp", bufs=6))
        psum = ctx.enter_context(tc.psum_pool(name="psum", bufs=1))

        ident = const.tile([P, P], F32, name="ident")
        make_identity(nc, ident[:])
        one = const.tile([P, 1], F32, name="one")
        nc.gpsimd.memset(one[:], 1.0)
        warm = const.tile([P, 1], F32, name="warm")
        nc.scalar.activation(out=warm[:], in_=one[:], func=ACT.Abs_reciprocal_sqrt)

        fv = features.rearrange("(a p j) k -> a p j k", p=P, j=4)
        ev = ex_features.rearrange("(a p j) k -> a p j k", p=P, j=4)
        o0 = out_0.rearrange("(a p j) f -> a p j f", p=P, j=4)
        o1 = out_1.rearrange("(a p j) f -> a p j f", p=P, j=4)
        n_f = fv.shape[0]
        n_groups = n_f + ev.shape[0]

        def src_group(a):
            return fv[a, :, :, :] if a < n_f else ev[a - n_f, :, :, :]

        def dst_group(a):
            return o0[a, :, :, :] if a < n_f else o1[a - n_f, :, :, :]

        ctx.enter_context(tc.manual_schedule())

        w_raw = []
        x_raw = {}
        x_shuf = {}
        x_pair = {}

        def bank_tile(pair, half):
            b = pair % 4 + 4 * half
            return psum.tile([P, NH], F32, name="bank%d" % b, offset=2048 * b)

        def load_w(f):
            if f % 2 == 1:
                return
            t = wpool.tile([P, 2, K], BF16, name="w_raw%d" % f)
            nc.sync.dma_start(out=t[:], in_=g_weight[f * P:(f + 2) * P, :].rearrange("(t p) k -> p t k", p=P))
            w_raw.append(t[:, 0, :])
            w_raw.append(t[:, 1, :])

        def load_x(a, halves):
            for h in halves:
                lo, hi = h
                t = xpool.tile([P, hi - lo, K], BF16, name="x_raw%d_%d" % (a, lo))
                nc.sync.dma_start(out=t[:], in_=src_group(a)[:, lo:hi, :])
                for s in range(lo, hi):
                    x_raw[(a, s)] = t[:, s - lo, :]
                    if s % 2 == 0:
                        x_pair[2 * a + s // 2] = t[:, s - lo:s - lo + 2, :]

        def transpose_rows(bank, rows):
            words = rows.bitcast(F32)
            for g in range(2):
                for u in range(2):
                    c = (2 * g + u) * P
                    nc.tensor.transpose(bank[:, c:c + P], words[:, 256 * g + u:256 * (g + 1):2], ident[:])

        def transpose_tile(bank, j, i):
            words = x_raw[(j // 2, 2 * (j % 2) + i)].bitcast(F32)
            for g in range(2):
                for u in range(2):
                    c = (2 * g + u) * P
                    if laid_out(j, i, g):
                        w0 = 384 * u + 256 * i + 128 * g - 128
                        nc.tensor.transpose(bank[:, c:c + P], x_shuf[j][:, w0:w0 + P], ident[:])
                    else:
                        nc.tensor.transpose(bank[:, c:c + P], words[:, 256 * g + u:256 * (g + 1):2], ident[:])

        def copy_out(on_scalar, dst, bank):
            src = bank[:].rearrange("p (g u r) -> p g r u", g=2, u=2)
            if on_scalar:
                nc.scalar.copy(out=dst, in_=src)
            else:
                nc.vector.tensor_copy(out=dst, in_=src)

        wg = [wpool.tile([P, 2, NH, 4], BF16, name="wg%d" % n, align_bytes=64) for n in range(2)]
        wc = [wpool.tile([P, 2, NH], U32, name="wc%d" % n, align_bytes=64) for n in range(2)]
        ws = [wpool.tile([P, 2, NH], U8, name="ws%d" % n, align_bytes=64) for n in range(2)]

        def quant_w(n, q):
            cols = slice(q * P, (q + 1) * P)
            for g in range(2):
                nc.vector.quantize_mx(
                    out=wc[n][:, g, cols].bitcast(E5X4),
                    scales=ws[n][:, g, cols],
                    in_=wg[n][:, g, cols, :].rearrange("p c t -> p (c t)"),
                )

        def prep_w(n):
            for q in range(4):
                f = 4 * n + q
                bank = bank_tile(W_PAIRS[f // 2], f % 2)
                transpose_rows(bank, w_raw[f])
                copy_out(q % 2 == 0, wg[n][:, :, q * P:(q + 1) * P, :].bitcast(F32), bank)
                if q >= 1:
                    quant_w(n, q - 1)
            quant_w(n, 3)

        pending = []

        def rsqrt_pending():
            for (j, i, acc) in pending:
                r = small.tile([P, 1], F32, name="r")
                nc.scalar.activation(out=r[:], in_=acc[:, 0:1], func=ACT.Abs_reciprocal_sqrt, bias=acc[:, 1:2])
                rs[(j, i)] = r
            pending.clear()

        xg = {}
        xq = {}
        banks = {}
        rs = {}
        ots = {}

        def shuffle_step(j):
            if j >= N_PAIRS:
                return
            if not laid_out(j, 1, 0):
                return
            sh = slots.tile([P, 8, P], F32, name="slot%d" % ((j - 2) % 3), align_bytes=64)
            words = sh[:].rearrange("p s w -> p (s w)")
            dst = words[:, 0:768].bitcast(BF16).rearrange("p (u v e) -> p u v e", u=2, e=2)
            src = x_pair[j].rearrange("p i k -> p (i k)").rearrange("p (v u e) -> p u v e", u=2, e=2)
            nc.gpsimd.tensor_scalar(out=dst, in0=src[:, :, 128:512, :], scalar1=1.0, scalar2=0.0, op0=ALU.mult, op1=ALU.add)
            x_shuf[j] = words

        def t_step(j):
            g_t = slots.tile([P, 2, 2, P, 4], BF16, name="slot%d" % (j % 3), align_bytes=64)
            xg[j] = g_t
            tbs = []
            for i in range(2):
                bank = bank_tile(j - 1, i)
                transpose_tile(bank, j, i)
                tbs.append(bank)
            for i in range(2):
                copy_out(copy_on_scalar(j, i), g_t[:, i, :, :, :].bitcast(F32), tbs[i])
                if i == 0:
                    rsqrt_pending()

        def q_step(j):
            c_t = qpool.tile([P, 4 * P], U32, name="xc", align_bytes=64)
            s_t = qpool.tile([P, 4 * P], U8, name="xs", align_bytes=64)
            nc.vector.quantize_mx(
                out=c_t[:].bitcast(E5X4),
                scales=s_t[:],
                in_=xg[j][:].rearrange("p i g r t -> p (i g r t)"),
            )
            xq[j] = (c_t, s_t)

        def m_step(j):
            c_t, s_t = xq[j]
            groups = [(i, n) for i in range(2) for n in range(2)]
            if j == 0:
                groups = [(i, n) for n in range(2) for i in range(2)]
            for (i, n) in groups:
                bank = bank_tile(j + 2 if (i == 0) != (j == N_PAIRS - 1) else j, n)
                banks[(j, i, n)] = bank
                for g in range(2):
                    cols = slice((2 * i + g) * P, (2 * i + g + 1) * P)
                    nc.tensor.matmul_mx(
                        out=bank[:],
                        lhsT=c_t[:, cols].bitcast(E5X4),
                        lhsT_scale=s_t[:, cols],
                        rhs=wc[n][:, g, :].bitcast(E5X4),
                        rhs_scale=ws[n][:, g, :],
                        start=(g == 0),
                        stop=(g == 1),
                    )

        def norm_step(j, i):
            acc = small.tile([P, 2], F32, name="acc")
            for n in range(2):
                junk = junkp.tile([P, NH], F32, name="junk")
                nc.scalar.activation(out=junk[:], in_=banks[(j, i, n)][:], func=ACT.Square, accum_out=acc[:, n:n + 1])
                if n == 0:
                    rsqrt_pending()
            pending.append((j, i, acc))

        def scale_step(j, i):
            if i == 0:
                ots[j] = outp.tile([P, 2, F], F32, name="ot")
            if any((j, i, n) in ON_SCALAR for n in range(2)):
                rc = small.tile([P, 1], F32, name="rc")
                nc.vector.tensor_scalar(out=rc[:], in0=rs[(j, i)][:, 0:1], scalar1=R_MAX, scalar2=None, op0=ALU.min)
            for n in range(2):
                if (j, i, n) in ON_SCALAR:
                    nc.scalar.activation(out=ots[j][:, i, n * NH:(n + 1) * NH], in_=banks[(j, i, n)][:], func=ACT.Copy, scale=rc[:, 0:1])
                    continue
                nc.vector.scalar_tensor_tensor(
                    out=ots[j][:, i, n * NH:(n + 1) * NH],
                    in0=rs[(j, i)][:, 0:1].to_broadcast([P, NH]),
                    scalar=R_MAX,
                    in1=banks[(j, i, n)][:],
                    op0=ALU.min,
                    op1=ALU.mult,
                )

        def store(j, lo, hi):
            s0 = 2 * (j % 2)
            nc.sync.dma_start(out=dst_group(j // 2)[:, s0 + lo:s0 + hi, :], in_=ots[j][:, lo:hi, :])

        for f in range(4):
            load_w(f)
        load_x(0, [(0, 2)])
        for f in range(4, 8):
            load_w(f)
        load_x(0, [(2, 4)])
        for a in range(1, PREFETCH):
            load_x(a, [(0, 4)])

        prep_w(0)
        t_step(0)
        q_step(0)
        prep_w(1)
        for j in range(1, AHEAD + 1):
            shuffle_step(j)

        for j in range(N_PAIRS):
            if j + 1 < N_PAIRS:
                t_step(j + 1)
            else:
                rsqrt_pending()
            if j >= 1:
                scale_step(j - 1, 0)
                if j >= FINE:
                    store(j - 1, 0, 1)
            if j + 1 < N_PAIRS:
                q_step(j + 1)
            if j >= 1:
                scale_step(j - 1, 1)
                if j >= FINE:
                    store(j - 1, 1, 2)
                else:
                    store(j - 1, 0, 2)
            if PREFETCH + j < n_groups:
                load_x(PREFETCH + j, [(0, 4)])
            shuffle_step(j + 1 + AHEAD)
            m_step(j)
            norm_step(j, 0)
            norm_step(j, 1)
        last = N_PAIRS - 1
        rsqrt_pending()
        scale_step(last, 0)
        store(last, 0, 1)
        scale_step(last, 1)
        store(last, 1, 2)
